import numpy as np
import ml_dtypes


def mxq(x, axis, fmt="e4m3"):
    dtype, down = {"e4m3": (ml_dtypes.float8_e4m3fn, 7), "e5m2": (ml_dtypes.float8_e5m2, 14)}[fmt]
    v = np.moveaxis(np.asarray(x, np.float32).astype(ml_dtypes.bfloat16).astype(np.float64), axis, -1)
    blocks = v.reshape(v.shape[:-1] + (-1, 32))
    amax = np.abs(blocks).max(-1, keepdims=True)
    byte = np.maximum(np.where(amax > 0, np.frexp(amax)[1] - 1 + 127, 0) - down, 1)
    scale = np.exp2(byte - 127.0)
    codes = (blocks / scale).astype(np.float32).astype(dtype).astype(np.float64)
    return np.moveaxis((codes * scale).reshape(v.shape), -1, axis)


WIDE = False


def mx_kscale(k):
    if not WIDE:
        return np.ones(k)
    levels = np.array([10, -10, 5, -5, 0])
    if k % 512:
        return np.exp2(np.random.permutation(np.resize(levels, k // 32))).repeat(32)
    a = np.empty((k // 512, 16))
    for p in range(k // 512):
        a[p, :8] = np.random.permutation(np.resize(levels, 8))
        for g in range(8):
            far = levels[np.abs(levels - a[p, g]) >= 10]
            a[p, g + 8] = far[np.random.randint(len(far))]
    return np.exp2(a.ravel()).repeat(32)


BF16 = ml_dtypes.bfloat16


def bf(x):
    return np.asarray(x, np.float32).astype(BF16)


def f64(x):
    return np.asarray(x).astype(np.float64)


B, CIN, HID, FREQ, T, H = 1, 512, 256, 4, 128, 8
HD = HID * FREQ // H
EPS = 1e-5


def setup_inputs():
    s = mx_kscale(CIN)
    return {"x": bf(np.random.standard_normal((B, CIN, FREQ, T)) * s[None, :, None, None]),
            "qkv_w": bf(np.random.standard_normal((3 * HID, CIN)) / np.sqrt(CIN) / s[None, :]),
            "qkv_b": bf(np.random.standard_normal(3 * HID) * 0.2),
            "qkv_alpha": bf(0.25 + 0.05 * np.random.standard_normal(1)),
            "qkv_gamma": bf(1.0 + 0.1 * np.random.standard_normal((1, 3 * HID, 1, FREQ))),
            "qkv_beta": bf(0.1 * np.random.standard_normal((1, 3 * HID, 1, FREQ)))}


def reference(x, qkv_w, qkv_b, qkv_alpha, qkv_gamma, qkv_beta):
    xt = np.swapaxes(f64(x), -2, -1)
    y = (mxq(f64(qkv_w), 1, "e4m3") @ mxq(xt, 1, "e4m3").reshape(B, CIN, T * FREQ)).reshape(B, 3 * HID, T, FREQ)
    y = y + f64(qkv_b)[None, :, None, None]
    y = np.where(y >= 0, y, f64(qkv_alpha)[0] * y)
    mu = y.mean(axis=(1, 3), keepdims=True)
    var = np.square(y - mu).mean(axis=(1, 3), keepdims=True)
    n = (y - mu) / np.sqrt(var + EPS) * f64(qkv_gamma) + f64(qkv_beta)
    n = np.swapaxes(np.swapaxes(n, 1, 2).reshape(B, T, H, 3 * HD), 1, 2)
    return (np.ascontiguousarray(n[..., :HD]), np.ascontiguousarray(n[..., HD:2 * HD]), np.ascontiguousarray(n[..., 2 * HD:]))

@@ -1,0 +1,297 @@
+from contextlib import ExitStack
+
+import concourse.mybir as mybir
+from concourse.masks import make_identity
+
+F32 = mybir.dt.float32
+BF16 = mybir.dt.bfloat16
+U32 = mybir.dt.uint32
+U8 = mybir.dt.uint8
+FP8X4 = mybir.dt.float8_e4m3fn_x4
+ALU = mybir.AluOpType
+ACT = mybir.ActivationFunctionType
+AXIS = mybir.AxisListType
+
+P = 128
+PACK = 4
+CIN = P * PACK
+FREQ = 4
+CHANNELS = 768
+O_TILES = CHANNELS // P
+BANK = P * FREQ
+COLS = CHANNELS * FREQ
+HEAD_DIM = 128
+UNITS_PER_BANK = BANK // HEAD_DIM
+EPS = 1e-5
+ROW_VALUES = 2 * P
+BIAS_ROWS = CHANNELS // ROW_VALUES
+GAIN_ROWS = COLS // ROW_VALUES
+ROWS_PER_BANK = BANK // P
+RUN = 4
+AHEAD = 3
+T_AHEAD = 4
+Q_AHEAD = 3
+
+FLOPS = 2 * CHANNELS * CIN * FREQ * P
+
+
+def tile_unified2dattentiononframe_pa_s_kernel(
+    tc, x, qkv_w, qkv_b, qkv_alpha, qkv_gamma, qkv_beta, out_0, out_1, out_2
+):
+    nc = tc.nc
+    out_views = [o.rearrange("a h t d -> t (a h) d") for o in (out_0, out_1, out_2)]
+
+    with ExitStack() as stack:
+        keep = stack.enter_context(tc.tile_pool(name="keep", bufs=1))
+        psum = stack.enter_context(tc.psum_pool(name="psum", bufs=8))
+        stack.enter_context(tc.manual_schedule())
+
+        def load_columns(queue, vec, n_rows, label):
+            columns = keep.tile([P, n_rows], F32, name=label)
+            queue.dma_start(
+                out=columns[:].bitcast(BF16).rearrange("w (r e) -> w r e", e=2),
+                in_=vec.rearrange("(r w e) -> w r e", w=P, e=2),
+            )
+            return columns
+
+        bias_cols = load_columns(nc.scalar, qkv_b, BIAS_ROWS, "bias_cols")
+        x_raw = keep.tile([P, PACK, BANK], BF16)
+        nc.sync.dma_start(
+            out=x_raw[:].rearrange("q s w -> q (s w)"),
+            in_=x.rearrange("a (q s) f t -> q (a s f t)", s=PACK),
+        )
+        w_raw = keep.tile([P, O_TILES, CIN], BF16)
+        w_rows = qkv_w.rearrange("(j r) c -> r j c", r=P)
+        for j in range(O_TILES):
+            nc.sync.dma_start(out=w_raw[:, j, :], in_=w_rows[:, j, :])
+
+        alpha_bc = keep.tile([P, 1], BF16)
+        nc.scalar.dma_start(out=alpha_bc[:], in_=qkv_alpha.partition_broadcast(P))
+        gamma_cols = load_columns(
+            nc.sync, qkv_gamma.rearrange("a o b f -> (a o b f)"), GAIN_ROWS, "gamma_cols"
+        )
+        beta_cols = load_columns(
+            nc.sync, qkv_beta.rearrange("a o b f -> (a o b f)"), GAIN_ROWS, "beta_cols"
+        )
+
+        ident = keep.tile([P, P], F32)
+        make_identity(nc, ident[:])
+        one = keep.tile([P, 1], F32)
+        nc.vector.memset(one[:], 1.0)
+        warm = keep.tile([P, 1], F32)
+        nc.scalar.activation(out=warm[:], in_=one[:], func=ACT.Sqrt)
+
+        x_grouped = keep.tile([P, BANK, PACK], BF16, align_bytes=64)
+        for f in range(FREQ):
+            cols = slice(f * P, (f + 1) * P)
+            dst = x_grouped[:, cols, :].rearrange("q (c i) s -> q c s i", i=RUN)
+            src = x_raw[:, :, cols].rearrange("q s (c i) -> q c s i", i=RUN)
+            if f < FREQ - 1:
+                nc.vector.tensor_copy(out=dst, in_=src)
+            else:
+                nc.scalar.copy(out=dst, in_=src)
+        x_codes = keep.tile([P, BANK], U32, align_bytes=64)
+        x_scales = keep.tile([P, BANK], U8, align_bytes=64)
+        nc.vector.quantize_mx(
+            out=x_codes[:].bitcast(FP8X4),
+            scales=x_scales[:],
+            in_=x_grouped[:].rearrange("q w s -> q (w s)"),
+        )
+
+        w_words = w_raw[:].rearrange("r j c -> r (j c)").bitcast(F32)
+        w_grouped = keep.tile([P, CHANNELS * PACK], BF16, align_bytes=64)
+        w_grouped_words = w_grouped[:].bitcast(F32).rearrange(
+            "q (j o u) -> q j o u", j=O_TILES, u=2
+        )
+        w_codes = keep.tile([P, CHANNELS], U32, align_bytes=64)
+        w_scales = keep.tile([P, CHANNELS], U8, align_bytes=64)
+
+        def transpose_w(j):
+            w_t = psum.tile([P, 2, P], F32, tag="bank")
+            for u in range(2):
+                words = w_words[:, j * (CIN // 2) + u : (j + 1) * (CIN // 2) : 2]
+                nc.tensor.transpose(w_t[:, u, :], words, ident[:])
+            nc.scalar.copy(
+                out=w_grouped_words[:, j, :, :], in_=w_t[:].rearrange("q u o -> q o u")
+            )
+
+        def spread_rows(bank, columns, first_row, n_rows):
+            for r in range(n_rows):
+                nc.tensor.transpose(
+                    bank[:, r * P : (r + 1) * P],
+                    columns[:, first_row + r : first_row + r + 1].to_broadcast([P, P]),
+                    ident[:],
+                )
+
+        bias_ps = psum.tile([P, BANK], F32, tag="bank")
+        spread_rows(bias_ps, bias_cols, 0, BIAS_ROWS)
+        bias_words = keep.tile([P, BIAS_ROWS * P], F32)
+        bias_bc = bias_words[:].bitcast(BF16)
+
+        def quantise_w(j):
+            nc.vector.quantize_mx(
+                out=w_codes[:, j * P : (j + 1) * P].bitcast(FP8X4),
+                scales=w_scales[:, j * P : (j + 1) * P],
+                in_=w_grouped[:, j * BANK : (j + 1) * BANK],
+            )
+
+        y = keep.tile([P, COLS], F32)
+        neg_part = keep.tile([P, COLS], F32)
+        prelu = keep.tile([P, COLS], F32)
+        squares = keep.tile([P, COLS], F32)
+        sum_p = keep.tile([P, O_TILES], F32)
+        sum_sq = keep.tile([P, O_TILES], F32)
+        neg_shift = keep.tile([P, 1], F32)
+        one_minus_alpha = keep.tile([P, 1], F32)
+        early_p = keep.tile([P, 1], F32)
+
+        products = {}
+
+        def multiply(j):
+            z = psum.tile([P, FREQ, P], F32, tag="bank")
+            for f in range(FREQ):
+                nc.tensor.matmul_mx(
+                    out=z[:, f, :],
+                    lhsT=x_codes[:, f * P : (f + 1) * P].bitcast(FP8X4),
+                    lhsT_scale=x_scales[:, f * P : (f + 1) * P],
+                    rhs=w_codes[:, j * P : (j + 1) * P].bitcast(FP8X4),
+                    rhs_scale=w_scales[:, j * P : (j + 1) * P],
+                    start=True,
+                    stop=True,
+                )
+            products[j] = z
+
+        def add_bias(j):
+            cols = slice(j * BANK, (j + 1) * BANK)
+            nc.vector.tensor_tensor(
+                out=y[:, cols].rearrange("t (o f) -> t o f", f=FREQ),
+                in0=products[j][:].rearrange("t f o -> t o f"),
+                in1=bias_bc[:, j * P : (j + 1) * P].unsqueeze(2).to_broadcast([P, P, FREQ]),
+                op=ALU.add,
+            )
+            nc.scalar.activation(
+                out=neg_part[:, cols], in_=y[:, cols], func=ACT.Relu, scale=-1.0
+            )
+
+        def activate(j):
+            cols = slice(j * BANK, (j + 1) * BANK)
+            nc.vector.scalar_tensor_tensor(
+                out=prelu[:, cols], in0=neg_part[:, cols], scalar=one_minus_alpha[:, 0:1],
+                in1=y[:, cols], op0=ALU.mult, op1=ALU.add, accum_out=sum_p[:, j : j + 1],
+            )
+            if j == 0:
+                nc.gpsimd.tensor_scalar(
+                    out=neg_shift[:], in0=sum_p[:, 0:1], scalar1=-1.0 / BANK, scalar2=0.0,
+                    op0=ALU.mult, op1=ALU.add,
+                )
+
+        def square(j):
+            cols = slice(j * BANK, (j + 1) * BANK)
+            nc.scalar.activation(
+                out=squares[:, cols], in_=prelu[:, cols], func=ACT.Square,
+                bias=neg_shift[:, 0:1], scale=1.0, accum_out=sum_sq[:, j : j + 1],
+            )
+
+        for j in range(T_AHEAD):
+            transpose_w(j)
+            if j == Q_AHEAD - 1:
+                nc.scalar.copy(out=bias_words[:], in_=bias_ps[:, 0 : BIAS_ROWS * P])
+        for j in range(Q_AHEAD):
+            quantise_w(j)
+        for s in range(O_TILES + 3):
+            if s < O_TILES:
+                multiply(s)
+            if s + T_AHEAD < O_TILES:
+                transpose_w(s + T_AHEAD)
+            if s < O_TILES:
+                add_bias(s)
+            if s + Q_AHEAD < O_TILES:
+                quantise_w(s + Q_AHEAD)
+            if s == 1:
+                nc.vector.tensor_scalar(
+                    out=one_minus_alpha[:], in0=alpha_bc[:], scalar1=-1.0, scalar2=1.0,
+                    op0=ALU.mult, op1=ALU.add,
+                )
+            if 2 <= s < O_TILES + 2:
+                activate(s - 2)
+            if s >= 3:
+                square(s - 3)
+
+        gamma_banks = []
+        beta_banks = []
+        for banks, columns, label in (
+            (gamma_banks, gamma_cols, "gamma"),
+            (beta_banks, beta_cols, "beta"),
+        ):
+            for k in range(GAIN_ROWS // ROWS_PER_BANK):
+                bank = psum.tile([P, BANK], F32, tag="bank", name="%s%d" % (label, k))
+                spread_rows(bank, columns, k * ROWS_PER_BANK, ROWS_PER_BANK)
+                banks.append(bank[:].bitcast(BF16))
+
+        centred = keep.tile([P, COLS], F32)
+        result = keep.tile([P, COLS], F32)
+        neg_mean = keep.tile([P, 1], F32)
+        offset = keep.tile([P, 1], F32)
+        neg_offset = keep.tile([P, 1], F32)
+        early_var = keep.tile([P, 1], F32)
+        early_sq = keep.tile([P, 1], F32)
+        rest = keep.tile([P, 1], F32)
+        std = keep.tile([P, 1], F32)
+        rstd = keep.tile([P, 1], F32)
+
+        def gain(c):
+            cols = slice(c * BANK, (c + 1) * BANK)
+            nc.vector.scalar_tensor_tensor(
+                out=centred[:, cols], in0=prelu[:, cols], scalar=neg_mean[:, 0:1],
+                in1=gamma_banks[c // 2][:, (c % 2) * BANK : (c % 2 + 1) * BANK],
+                op0=ALU.add, op1=ALU.mult,
+            )
+
+        def shift_and_store(c):
+            cols = slice(c * BANK, (c + 1) * BANK)
+            nc.vector.scalar_tensor_tensor(
+                out=result[:, cols], in0=centred[:, cols], scalar=rstd[:, 0:1],
+                in1=beta_banks[c // 2][:, (c % 2) * BANK : (c % 2 + 1) * BANK],
+                op0=ALU.mult, op1=ALU.add,
+            )
+            for g in range(c * UNITS_PER_BANK, (c + 1) * UNITS_PER_BANK):
+                nc.sync.dma_start(
+                    out=out_views[g % 3][:, g // 3, :],
+                    in_=result[:, g * HEAD_DIM : (g + 1) * HEAD_DIM],
+                )
+
+        last = O_TILES - 1
+        nc.vector.tensor_reduce(out=early_p[:], in_=sum_p[:, 0:last], axis=AXIS.X, op=ALU.add)
+        nc.vector.tensor_scalar(
+            out=neg_mean[:], in0=sum_p[:, last : last + 1], scalar1=early_p[:, 0:1],
+            scalar2=-1.0 / COLS, op0=ALU.add, op1=ALU.mult,
+        )
+        gain(0)
+        nc.vector.tensor_reduce(
+            out=early_sq[:], in_=sum_sq[:, 0:last], axis=AXIS.X, op=ALU.add
+        )
+        nc.vector.tensor_tensor(
+            out=offset[:], in0=neg_shift[:], in1=neg_mean[:], op=ALU.subtract
+        )
+        nc.vector.tensor_tensor(
+            out=neg_offset[:], in0=neg_mean[:], in1=neg_shift[:], op=ALU.subtract
+        )
+        nc.vector.tensor_scalar(
+            out=early_var[:], in0=early_sq[:], scalar1=1.0 / COLS, scalar2=EPS,
+            op0=ALU.mult, op1=ALU.add,
+        )
+        gain(1)
+        nc.vector.scalar_tensor_tensor(
+            out=rest[:], in0=offset[:], scalar=neg_offset[:, 0:1], in1=early_var[:],
+            op0=ALU.mult, op1=ALU.add,
+        )
+        nc.scalar.activation(
+            out=std[:], in_=sum_sq[:, last : last + 1], func=ACT.Sqrt,
+            bias=rest[:, 0:1], scale=1.0 / COLS,
+        )
+        gain(2)
+        nc.vector.reciprocal(out=rstd[:], in_=std[:])
+        for c in range(O_TILES):
+            if AHEAD <= c + 1 < O_TILES:
+                gain(c + 1)
+            shift_and_store(c)

@@ -21,14 +21,17 @@ O_TILES = CHANNELS // P
 BANK = P * FREQ
 COLS = CHANNELS * FREQ
 HEAD_DIM = 128
-UNITS_PER_BANK = BANK // HEAD_DIM
 EPS = 1e-5
 ROW_VALUES = 2 * P
 BIAS_ROWS = CHANNELS // ROW_VALUES
 GAIN_ROWS = COLS // ROW_VALUES
-ROWS_PER_BANK = BANK // P
+HEADS = 8
+HEAD = COLS // HEADS
+PAIR = 2 * HEAD
+PAIRS = HEADS // 2
+ROWS_PER_PAIR = PAIR // ROW_VALUES
 RUN = 4
-AHEAD = 3
+SIDE = 1024
 T_AHEAD = 4
 Q_AHEAD = 3
 
@@ -81,6 +84,27 @@ def tile_unified2dattentiononframe_pa_s_kernel(
         warm = keep.tile([P, 1], F32)
         nc.scalar.activation(out=warm[:], in_=one[:], func=ACT.Sqrt)
 
+        flag = keep.tile([P, 1], F32)
+        nc.gpsimd.tensor_scalar(
+            out=flag[:], in0=alpha_bc[:], scalar1=1.0, scalar2=-2.0,
+            op0=ALU.is_gt, op1=ALU.mult,
+        )
+        sign = keep.tile([P, 1], F32)
+        nc.gpsimd.tensor_scalar(
+            out=sign[:], in0=flag[:], scalar1=1.0, scalar2=1.0, op0=ALU.add, op1=ALU.mult,
+        )
+
+        def signed_columns(columns, n_rows, label):
+            signed = keep.tile([P, n_rows], F32, name=label)
+            nc.gpsimd.tensor_scalar(
+                out=signed[:].bitcast(BF16), in0=columns[:].bitcast(BF16),
+                scalar1=sign[:, 0:1], scalar2=0.0, op0=ALU.mult, op1=ALU.add,
+            )
+            return signed
+
+        bias_signed = signed_columns(bias_cols, BIAS_ROWS, "bias_signed")
+        gamma_signed = signed_columns(gamma_cols, GAIN_ROWS, "gamma_signed")
+
         x_grouped = keep.tile([P, BANK, PACK], BF16, align_bytes=64)
         for f in range(FREQ):
             cols = slice(f * P, (f + 1) * P)
@@ -123,8 +147,6 @@ def tile_unified2dattentiononframe_pa_s_kernel(
                     ident[:],
                 )
 
-        bias_ps = psum.tile([P, BANK], F32, tag="bank")
-        spread_rows(bias_ps, bias_cols, 0, BIAS_ROWS)
         bias_words = keep.tile([P, BIAS_ROWS * P], F32)
         bias_bc = bias_words[:].bitcast(BF16)
 
@@ -136,13 +158,16 @@ def tile_unified2dattentiononframe_pa_s_kernel(
             )
 
         y = keep.tile([P, COLS], F32)
-        neg_part = keep.tile([P, COLS], F32)
         prelu = keep.tile([P, COLS], F32)
         squares = keep.tile([P, COLS], F32)
         sum_p = keep.tile([P, O_TILES], F32)
-        sum_sq = keep.tile([P, O_TILES], F32)
+        sum_sq = keep.tile([P, O_TILES + 1], F32)
+        nc.vector.tensor_scalar(
+            out=sum_sq[:, 0:1], in0=one[:], scalar1=COLS * EPS, scalar2=0.0,
+            op0=ALU.mult, op1=ALU.add,
+        )
         neg_shift = keep.tile([P, 1], F32)
-        one_minus_alpha = keep.tile([P, 1], F32)
+        shift = keep.tile([P, 1], F32)
         early_p = keep.tile([P, 1], F32)
 
         products = {}
@@ -163,135 +188,152 @@ def tile_unified2dattentiononframe_pa_s_kernel(
 
         def add_bias(j):
             cols = slice(j * BANK, (j + 1) * BANK)
-            nc.vector.tensor_tensor(
+            nc.vector.scalar_tensor_tensor(
                 out=y[:, cols].rearrange("t (o f) -> t o f", f=FREQ),
-                in0=products[j][:].rearrange("t f o -> t o f"),
+                in0=products[j][:].rearrange("t f o -> t o f"), scalar=sign[:, 0:1],
                 in1=bias_bc[:, j * P : (j + 1) * P].unsqueeze(2).to_broadcast([P, P, FREQ]),
-                op=ALU.add,
-            )
-            nc.scalar.activation(
-                out=neg_part[:, cols], in_=y[:, cols], func=ACT.Relu, scale=-1.0
+                op0=ALU.mult, op1=ALU.add,
             )
 
         def activate(j):
             cols = slice(j * BANK, (j + 1) * BANK)
             nc.vector.scalar_tensor_tensor(
-                out=prelu[:, cols], in0=neg_part[:, cols], scalar=one_minus_alpha[:, 0:1],
-                in1=y[:, cols], op0=ALU.mult, op1=ALU.add, accum_out=sum_p[:, j : j + 1],
+                out=prelu[:, cols], in0=y[:, cols], scalar=alpha_bc[:, 0:1],
+                in1=y[:, cols], op0=ALU.mult, op1=ALU.max, accum_out=sum_p[:, j : j + 1],
             )
             if j == 0:
-                nc.gpsimd.tensor_scalar(
-                    out=neg_shift[:], in0=sum_p[:, 0:1], scalar1=-1.0 / BANK, scalar2=0.0,
-                    op0=ALU.mult, op1=ALU.add,
+                nc.scalar.activation(
+                    out=neg_shift[:], in_=sum_p[:, 0:1], func=ACT.Copy, scale=-1.0 / BANK,
+                )
+                nc.scalar.activation(
+                    out=shift[:], in_=sum_p[:, 0:1], func=ACT.Copy, scale=1.0 / BANK,
                 )
 
         def square(j):
             cols = slice(j * BANK, (j + 1) * BANK)
             nc.scalar.activation(
                 out=squares[:, cols], in_=prelu[:, cols], func=ACT.Square,
-                bias=neg_shift[:, 0:1], scale=1.0, accum_out=sum_sq[:, j : j + 1],
+                bias=neg_shift[:, 0:1], scale=1.0, accum_out=sum_sq[:, j + 1 : j + 2],
             )
 
         for j in range(T_AHEAD):
             transpose_w(j)
             if j == Q_AHEAD - 1:
+                bias_ps = psum.tile([P, BANK], F32, tag="bank")
+                spread_rows(bias_ps, bias_signed, 0, BIAS_ROWS)
                 nc.scalar.copy(out=bias_words[:], in_=bias_ps[:, 0 : BIAS_ROWS * P])
         for j in range(Q_AHEAD):
             quantise_w(j)
-        for s in range(O_TILES + 3):
+        gamma_banks = []
+        beta_banks = []
+
+        def spread_gain_and_shift():
+            for banks, columns, label in (
+                (gamma_banks, gamma_signed, "gamma"),
+                (beta_banks, beta_cols, "beta"),
+            ):
+                for k in range(PAIRS):
+                    bank = psum.tile([P, BANK], F32, tag="bank", name="%s%d" % (label, k))
+                    spread_rows(bank, columns, k * ROWS_PER_PAIR, ROWS_PER_PAIR)
+                    banks.append(bank[:, 0 : PAIR // 2])
+
+        side_gamma = keep.tile([P, SIDE // 2], F32)
+
+        def copy_side_gamma():
+            whole = PAIR // 2
+            part = SIDE // 2 - whole
+            nc.scalar.copy(out=side_gamma[:, 0:part], in_=gamma_banks[-2][:, whole - part : whole])
+            nc.scalar.copy(out=side_gamma[:, part:], in_=gamma_banks[-1])
+
+        for s in range(O_TILES + 2):
             if s < O_TILES:
                 multiply(s)
             if s + T_AHEAD < O_TILES:
                 transpose_w(s + T_AHEAD)
+            if s == O_TILES - 1:
+                spread_gain_and_shift()
             if s < O_TILES:
                 add_bias(s)
             if s + Q_AHEAD < O_TILES:
                 quantise_w(s + Q_AHEAD)
-            if s == 1:
-                nc.vector.tensor_scalar(
-                    out=one_minus_alpha[:], in0=alpha_bc[:], scalar1=-1.0, scalar2=1.0,
-                    op0=ALU.mult, op1=ALU.add,
+            if s == O_TILES:
+                nc.vector.tensor_reduce(
+                    out=early_p[:], in_=sum_p[:, 0 : O_TILES - 1], axis=AXIS.X, op=ALU.add
                 )
-            if 2 <= s < O_TILES + 2:
-                activate(s - 2)
-            if s >= 3:
-                square(s - 3)
-
-        gamma_banks = []
-        beta_banks = []
-        for banks, columns, label in (
-            (gamma_banks, gamma_cols, "gamma"),
-            (beta_banks, beta_cols, "beta"),
-        ):
-            for k in range(GAIN_ROWS // ROWS_PER_BANK):
-                bank = psum.tile([P, BANK], F32, tag="bank", name="%s%d" % (label, k))
-                spread_rows(bank, columns, k * ROWS_PER_BANK, ROWS_PER_BANK)
-                banks.append(bank[:].bitcast(BF16))
+            if 1 <= s < O_TILES + 1:
+                activate(s - 1)
+            if s >= 2:
+                square(s - 2)
+            if s == O_TILES - 1:
+                copy_side_gamma()
 
         centred = keep.tile([P, COLS], F32)
         result = keep.tile([P, COLS], F32)
         neg_mean = keep.tile([P, 1], F32)
-        offset = keep.tile([P, 1], F32)
-        neg_offset = keep.tile([P, 1], F32)
-        early_var = keep.tile([P, 1], F32)
+        offset_sq = keep.tile([P, 1], F32)
         early_sq = keep.tile([P, 1], F32)
         rest = keep.tile([P, 1], F32)
         std = keep.tile([P, 1], F32)
         rstd = keep.tile([P, 1], F32)
+        offsets = keep.tile([P, SIDE], F32)
+        side_start = COLS - SIDE
 
-        def gain(c):
-            cols = slice(c * BANK, (c + 1) * BANK)
+        def gain(first, end):
+            pair = first // PAIR
+            words = gamma_banks[pair].bitcast(BF16)
             nc.vector.scalar_tensor_tensor(
-                out=centred[:, cols], in0=prelu[:, cols], scalar=neg_mean[:, 0:1],
-                in1=gamma_banks[c // 2][:, (c % 2) * BANK : (c % 2 + 1) * BANK],
+                out=centred[:, first:end], in0=prelu[:, first:end], scalar=neg_mean[:, 0:1],
+                in1=words[:, first - pair * PAIR : end - pair * PAIR],
                 op0=ALU.add, op1=ALU.mult,
             )
 
-        def shift_and_store(c):
-            cols = slice(c * BANK, (c + 1) * BANK)
+        def gain_beside(first, end):
+            side = slice(first - side_start, end - side_start)
+            nc.scalar.activation(
+                out=offsets[:, side], in_=prelu[:, first:end],
+                func=ACT.Identity, bias=neg_mean[:, 0:1], scale=1.0,
+            )
+            nc.gpsimd.tensor_tensor(
+                out=centred[:, first:end], in0=offsets[:, side],
+                in1=side_gamma[:].bitcast(BF16)[:, side], op=ALU.mult,
+            )
+
+        def shift_and_store(pair):
+            cols = slice(pair * PAIR, (pair + 1) * PAIR)
             nc.vector.scalar_tensor_tensor(
                 out=result[:, cols], in0=centred[:, cols], scalar=rstd[:, 0:1],
-                in1=beta_banks[c // 2][:, (c % 2) * BANK : (c % 2 + 1) * BANK],
-                op0=ALU.mult, op1=ALU.add,
+                in1=beta_banks[pair].bitcast(BF16), op0=ALU.mult, op1=ALU.add,
             )
-            for g in range(c * UNITS_PER_BANK, (c + 1) * UNITS_PER_BANK):
+            by_kind = result[:, cols].rearrange("t (h k d) -> t k h d", h=2, k=3)
+            for k in range(3):
                 nc.sync.dma_start(
-                    out=out_views[g % 3][:, g // 3, :],
-                    in_=result[:, g * HEAD_DIM : (g + 1) * HEAD_DIM],
+                    out=out_views[k][:, 2 * pair : 2 * pair + 2, :], in_=by_kind[:, k, :, :]
                 )
 
         last = O_TILES - 1
-        nc.vector.tensor_reduce(out=early_p[:], in_=sum_p[:, 0:last], axis=AXIS.X, op=ALU.add)
         nc.vector.tensor_scalar(
             out=neg_mean[:], in0=sum_p[:, last : last + 1], scalar1=early_p[:, 0:1],
             scalar2=-1.0 / COLS, op0=ALU.add, op1=ALU.mult,
         )
-        gain(0)
         nc.vector.tensor_reduce(
-            out=early_sq[:], in_=sum_sq[:, 0:last], axis=AXIS.X, op=ALU.add
-        )
-        nc.vector.tensor_tensor(
-            out=offset[:], in0=neg_shift[:], in1=neg_mean[:], op=ALU.subtract
-        )
-        nc.vector.tensor_tensor(
-            out=neg_offset[:], in0=neg_mean[:], in1=neg_shift[:], op=ALU.subtract
-        )
-        nc.vector.tensor_scalar(
-            out=early_var[:], in0=early_sq[:], scalar1=1.0 / COLS, scalar2=EPS,
-            op0=ALU.mult, op1=ALU.add,
-        )
-        gain(1)
-        nc.vector.scalar_tensor_tensor(
-            out=rest[:], in0=offset[:], scalar=neg_offset[:, 0:1], in1=early_var[:],
-            op0=ALU.mult, op1=ALU.add,
+            out=early_sq[:], in_=sum_sq[:, 0 : last + 1], axis=AXIS.X, op=ALU.add
         )
         nc.scalar.activation(
-            out=std[:], in_=sum_sq[:, last : last + 1], func=ACT.Sqrt,
+            out=offset_sq[:], in_=neg_mean[:], func=ACT.Square, bias=shift[:, 0:1], scale=1.0
+        )
+        gain(0, PAIR)
+        gain_beside(side_start, COLS - PAIR)
+        nc.vector.scalar_tensor_tensor(
+            out=rest[:], in0=early_sq[:], scalar=1.0 / COLS, in1=offset_sq[:],
+            op0=ALU.mult, op1=ALU.subtract,
+        )
+        nc.scalar.activation(
+            out=std[:], in_=sum_sq[:, last + 1 : last + 2], func=ACT.Sqrt,
             bias=rest[:, 0:1], scale=1.0 / COLS,
         )
-        gain(2)
+        gain(PAIR, 2 * PAIR)
+        gain_beside(COLS - PAIR, COLS)
         nc.vector.reciprocal(out=rstd[:], in_=std[:])
-        for c in range(O_TILES):
-            if AHEAD <= c + 1 < O_TILES:
-                gain(c + 1)
-            shift_and_store(c)
+        gain(2 * PAIR, side_start)
+        for pair in range(PAIRS):
+            shift_and_store(pair)

@@ -31,9 +31,8 @@ PAIR = 2 * HEAD
 PAIRS = HEADS // 2
 ROWS_PER_PAIR = PAIR // ROW_VALUES
 RUN = 4
-SIDE = 1024
-T_AHEAD = 4
-Q_AHEAD = 3
+T_AHEAD = 3
+Q_AHEAD = 2
 
 FLOPS = 2 * CHANNELS * CIN * FREQ * P
 
@@ -57,19 +56,20 @@ def tile_unified2dattentiononframe_pa_s_kernel(
             )
             return columns
 
-        bias_cols = load_columns(nc.scalar, qkv_b, BIAS_ROWS, "bias_cols")
-        x_raw = keep.tile([P, PACK, BANK], BF16)
-        nc.sync.dma_start(
-            out=x_raw[:].rearrange("q s w -> q (s w)"),
-            in_=x.rearrange("a (q s) f t -> q (a s f t)", s=PACK),
-        )
-        w_raw = keep.tile([P, O_TILES, CIN], BF16)
-        w_rows = qkv_w.rearrange("(j r) c -> r j c", r=P)
-        for j in range(O_TILES):
-            nc.sync.dma_start(out=w_raw[:, j, :], in_=w_rows[:, j, :])
-
         alpha_bc = keep.tile([P, 1], BF16)
         nc.scalar.dma_start(out=alpha_bc[:], in_=qkv_alpha.partition_broadcast(P))
+        bias_cols = load_columns(nc.scalar, qkv_b, BIAS_ROWS, "bias_cols")
+        x_raw = keep.tile([P, PACK, BANK], BF16)
+        x_rows = x.rearrange("a (q s) f t -> q (a s) (f t)", s=PACK)
+        w_raw = keep.tile([P, O_TILES, CIN], BF16)
+        w_rows = qkv_w.rearrange("(j r) c -> r j c", r=P)
+        nc.sync.dma_start(out=w_raw[:, 0, :], in_=w_rows[:, 0, :])
+        for half in range(2):
+            cols = slice(half * BANK // 2, (half + 1) * BANK // 2)
+            nc.sync.dma_start(out=x_raw[:, :, cols], in_=x_rows[:, :, cols])
+        for j in range(1, O_TILES):
+            nc.sync.dma_start(out=w_raw[:, j, :], in_=w_rows[:, j, :])
+
         gamma_cols = load_columns(
             nc.sync, qkv_gamma.rearrange("a o b f -> (a o b f)"), GAIN_ROWS, "gamma_cols"
         )
@@ -84,29 +84,30 @@ def tile_unified2dattentiononframe_pa_s_kernel(
         warm = keep.tile([P, 1], F32)
         nc.scalar.activation(out=warm[:], in_=one[:], func=ACT.Sqrt)
 
-        flag = keep.tile([P, 1], F32)
-        nc.gpsimd.tensor_scalar(
-            out=flag[:], in0=alpha_bc[:], scalar1=1.0, scalar2=-2.0,
-            op0=ALU.is_gt, op1=ALU.mult,
-        )
         sign = keep.tile([P, 1], F32)
-        nc.gpsimd.tensor_scalar(
-            out=sign[:], in0=flag[:], scalar1=1.0, scalar2=1.0, op0=ALU.add, op1=ALU.mult,
+        one_plus = keep.tile([P, 1], F32)
+        nc.vector.tensor_scalar(
+            out=one_plus[:], in0=one[:], scalar1=1.001, scalar2=0.0, op0=ALU.mult, op1=ALU.add
+        )
+        nc.scalar.activation(
+            out=sign[:], in_=alpha_bc[:], func=ACT.Sign, bias=one_plus[:, 0:1], scale=-1.0
         )
 
         def signed_columns(columns, n_rows, label):
             signed = keep.tile([P, n_rows], F32, name=label)
-            nc.gpsimd.tensor_scalar(
-                out=signed[:].bitcast(BF16), in0=columns[:].bitcast(BF16),
-                scalar1=sign[:, 0:1], scalar2=0.0, op0=ALU.mult, op1=ALU.add,
+            nc.scalar.activation(
+                out=signed[:].bitcast(BF16), in_=columns[:].bitcast(BF16), func=ACT.Copy,
+                scale=sign[:, 0:1],
             )
             return signed
 
         bias_signed = signed_columns(bias_cols, BIAS_ROWS, "bias_signed")
-        gamma_signed = signed_columns(gamma_cols, GAIN_ROWS, "gamma_signed")
 
         x_grouped = keep.tile([P, BANK, PACK], BF16, align_bytes=64)
-        for f in range(FREQ):
+        x_codes = keep.tile([P, BANK], U32, align_bytes=64)
+        x_scales = keep.tile([P, BANK], U8, align_bytes=64)
+
+        def group_x(f):
             cols = slice(f * P, (f + 1) * P)
             dst = x_grouped[:, cols, :].rearrange("q (c i) s -> q c s i", i=RUN)
             src = x_raw[:, :, cols].rearrange("q s (c i) -> q c s i", i=RUN)
@@ -114,13 +115,14 @@ def tile_unified2dattentiononframe_pa_s_kernel(
                 nc.vector.tensor_copy(out=dst, in_=src)
             else:
                 nc.scalar.copy(out=dst, in_=src)
-        x_codes = keep.tile([P, BANK], U32, align_bytes=64)
-        x_scales = keep.tile([P, BANK], U8, align_bytes=64)
-        nc.vector.quantize_mx(
-            out=x_codes[:].bitcast(FP8X4),
-            scales=x_scales[:],
-            in_=x_grouped[:].rearrange("q w s -> q (w s)"),
-        )
+
+        def quantise_x(half):
+            cols = slice(half * BANK // 2, (half + 1) * BANK // 2)
+            nc.vector.quantize_mx(
+                out=x_codes[:, cols].bitcast(FP8X4),
+                scales=x_scales[:, cols],
+                in_=x_grouped[:, cols, :].rearrange("q w s -> q (w s)"),
+            )
 
         w_words = w_raw[:].rearrange("r j c -> r (j c)").bitcast(F32)
         w_grouped = keep.tile([P, CHANNELS * PACK], BF16, align_bytes=64)
@@ -216,18 +218,24 @@ def tile_unified2dattentiononframe_pa_s_kernel(
                 bias=neg_shift[:, 0:1], scale=1.0, accum_out=sum_sq[:, j + 1 : j + 2],
             )
 
-        for j in range(T_AHEAD):
+        group_x(0)
+        group_x(1)
+        for j in range(T_AHEAD - 1):
             transpose_w(j)
-            if j == Q_AHEAD - 1:
+            if j == 0:
+                group_x(FREQ - 1)
                 bias_ps = psum.tile([P, BANK], F32, tag="bank")
                 spread_rows(bias_ps, bias_signed, 0, BIAS_ROWS)
                 nc.scalar.copy(out=bias_words[:], in_=bias_ps[:, 0 : BIAS_ROWS * P])
-        for j in range(Q_AHEAD):
-            quantise_w(j)
+        quantise_w(0)
+        group_x(2)
+        quantise_x(0)
+        quantise_x(1)
+        quantise_w(1)
         gamma_banks = []
         beta_banks = []
 
-        def spread_gain_and_shift():
+        def spread_gain_and_shift(gamma_signed):
             for banks, columns, label in (
                 (gamma_banks, gamma_signed, "gamma"),
                 (beta_banks, beta_cols, "beta"),
@@ -237,21 +245,17 @@ def tile_unified2dattentiononframe_pa_s_kernel(
                     spread_rows(bank, columns, k * ROWS_PER_PAIR, ROWS_PER_PAIR)
                     banks.append(bank[:, 0 : PAIR // 2])
 
-        side_gamma = keep.tile([P, SIDE // 2], F32)
-
-        def copy_side_gamma():
-            whole = PAIR // 2
-            part = SIDE // 2 - whole
-            nc.scalar.copy(out=side_gamma[:, 0:part], in_=gamma_banks[-2][:, whole - part : whole])
-            nc.scalar.copy(out=side_gamma[:, part:], in_=gamma_banks[-1])
-
         for s in range(O_TILES + 2):
+            if s == 3:
+                gamma_signed = signed_columns(gamma_cols, GAIN_ROWS, "gamma_signed")
             if s < O_TILES:
                 multiply(s)
+            if s == 0:
+                transpose_w(T_AHEAD - 1)
             if s + T_AHEAD < O_TILES:
                 transpose_w(s + T_AHEAD)
             if s == O_TILES - 1:
-                spread_gain_and_shift()
+                spread_gain_and_shift(gamma_signed)
             if s < O_TILES:
                 add_bias(s)
             if s + Q_AHEAD < O_TILES:
@@ -264,8 +268,6 @@ def tile_unified2dattentiononframe_pa_s_kernel(
                 activate(s - 1)
             if s >= 2:
                 square(s - 2)
-            if s == O_TILES - 1:
-                copy_side_gamma()
 
         centred = keep.tile([P, COLS], F32)
         result = keep.tile([P, COLS], F32)
@@ -275,8 +277,6 @@ def tile_unified2dattentiononframe_pa_s_kernel(
         rest = keep.tile([P, 1], F32)
         std = keep.tile([P, 1], F32)
         rstd = keep.tile([P, 1], F32)
-        offsets = keep.tile([P, SIDE], F32)
-        side_start = COLS - SIDE
 
         def gain(first, end):
             pair = first // PAIR
@@ -285,17 +285,6 @@ def tile_unified2dattentiononframe_pa_s_kernel(
                 out=centred[:, first:end], in0=prelu[:, first:end], scalar=neg_mean[:, 0:1],
                 in1=words[:, first - pair * PAIR : end - pair * PAIR],
                 op0=ALU.add, op1=ALU.mult,
-            )
-
-        def gain_beside(first, end):
-            side = slice(first - side_start, end - side_start)
-            nc.scalar.activation(
-                out=offsets[:, side], in_=prelu[:, first:end],
-                func=ACT.Identity, bias=neg_mean[:, 0:1], scale=1.0,
-            )
-            nc.gpsimd.tensor_tensor(
-                out=centred[:, first:end], in0=offsets[:, side],
-                in1=side_gamma[:].bitcast(BF16)[:, side], op=ALU.mult,
             )
 
         def shift_and_store(pair):
@@ -322,7 +311,6 @@ def tile_unified2dattentiononframe_pa_s_kernel(
             out=offset_sq[:], in_=neg_mean[:], func=ACT.Square, bias=shift[:, 0:1], scale=1.0
         )
         gain(0, PAIR)
-        gain_beside(side_start, COLS - PAIR)
         nc.vector.scalar_tensor_tensor(
             out=rest[:], in0=early_sq[:], scalar=1.0 / COLS, in1=offset_sq[:],
             op0=ALU.mult, op1=ALU.subtract,
@@ -332,8 +320,12 @@ def tile_unified2dattentiononframe_pa_s_kernel(
             bias=rest[:, 0:1], scale=1.0 / COLS,
         )
         gain(PAIR, 2 * PAIR)
-        gain_beside(COLS - PAIR, COLS)
         nc.vector.reciprocal(out=rstd[:], in_=std[:])
-        gain(2 * PAIR, side_start)
-        for pair in range(PAIRS):
-            shift_and_store(pair)
+        gain(2 * PAIR, 2 * PAIR + HEAD)
+        shift_and_store(0)
+        gain(2 * PAIR + HEAD, 3 * PAIR)
+        shift_and_store(1)
+        gain(3 * PAIR, 3 * PAIR + HEAD)
+        shift_and_store(2)
+        gain(3 * PAIR + HEAD, 4 * PAIR)
+        shift_and_store(3)

@@ -31,6 +31,9 @@ PAIR = 2 * HEAD
 PAIRS = HEADS // 2
 ROWS_PER_PAIR = PAIR // ROW_VALUES
 RUN = 4
+WARM_PRODUCTS = 3
+WARM_COLS = 256
+KEEP_WARM_COLS = 64
 T_AHEAD = 3
 Q_AHEAD = 2
 
@@ -82,7 +85,7 @@ def tile_unified2dattentiononframe_pa_s_kernel(
         one = keep.tile([P, 1], F32)
         nc.vector.memset(one[:], 1.0)
         warm = keep.tile([P, 1], F32)
-        nc.scalar.activation(out=warm[:], in_=one[:], func=ACT.Sqrt)
+        nc.scalar.activation(out=warm[:], in_=one[:], func=ACT.Abs_reciprocal_sqrt)
 
         sign = keep.tile([P, 1], F32)
         one_plus = keep.tile([P, 1], F32)
@@ -102,6 +105,18 @@ def tile_unified2dattentiononframe_pa_s_kernel(
             return signed
 
         bias_signed = signed_columns(bias_cols, BIAS_ROWS, "bias_signed")
+
+        zeros = keep.tile([P, WARM_COLS], F32)
+        nc.vector.memset(zeros[:], 0.0)
+
+        def idle_product(out):
+            nc.tensor.matmul(
+                out, lhsT=zeros[:, 0:P], rhs=zeros[:, 0 : out.shape[1]], start=True, stop=True
+            )
+
+        warm_ps = psum.tile([P, BANK], F32, tag="bank")
+        for k in range(WARM_PRODUCTS):
+            idle_product(warm_ps[:, 0:WARM_COLS])
 
         x_grouped = keep.tile([P, BANK, PACK], BF16, align_bytes=64)
         x_codes = keep.tile([P, BANK], U32, align_bytes=64)
@@ -133,12 +148,13 @@ def tile_unified2dattentiononframe_pa_s_kernel(
         w_scales = keep.tile([P, CHANNELS], U8, align_bytes=64)
 
         def transpose_w(j):
-            w_t = psum.tile([P, 2, P], F32, tag="bank")
+            w_t = psum.tile([P, 4, P], F32, tag="bank")
             for u in range(2):
                 words = w_words[:, j * (CIN // 2) + u : (j + 1) * (CIN // 2) : 2]
                 nc.tensor.transpose(w_t[:, u, :], words, ident[:])
+            idle_product(w_t[:, 2, 0:KEEP_WARM_COLS])
             nc.scalar.copy(
-                out=w_grouped_words[:, j, :, :], in_=w_t[:].rearrange("q u o -> q o u")
+                out=w_grouped_words[:, j, :, :], in_=w_t[:, 0:2, :].rearrange("q u o -> q o u")
             )
 
         def spread_rows(bank, columns, first_row, n_rows):
@@ -235,9 +251,9 @@ def tile_unified2dattentiononframe_pa_s_kernel(
         gamma_banks = []
         beta_banks = []
 
-        def spread_gain_and_shift(gamma_signed):
+        def spread_gain_and_shift():
             for banks, columns, label in (
-                (gamma_banks, gamma_signed, "gamma"),
+                (gamma_banks, gamma_cols, "gamma"),
                 (beta_banks, beta_cols, "beta"),
             ):
                 for k in range(PAIRS):
@@ -246,8 +262,6 @@ def tile_unified2dattentiononframe_pa_s_kernel(
                     banks.append(bank[:, 0 : PAIR // 2])
 
         for s in range(O_TILES + 2):
-            if s == 3:
-                gamma_signed = signed_columns(gamma_cols, GAIN_ROWS, "gamma_signed")
             if s < O_TILES:
                 multiply(s)
             if s == 0:
@@ -255,7 +269,7 @@ def tile_unified2dattentiononframe_pa_s_kernel(
             if s + T_AHEAD < O_TILES:
                 transpose_w(s + T_AHEAD)
             if s == O_TILES - 1:
-                spread_gain_and_shift(gamma_signed)
+                spread_gain_and_shift()
             if s < O_TILES:
                 add_bias(s)
             if s + Q_AHEAD < O_TILES:
@@ -275,7 +289,7 @@ def tile_unified2dattentiononframe_pa_s_kernel(
         offset_sq = keep.tile([P, 1], F32)
         early_sq = keep.tile([P, 1], F32)
         rest = keep.tile([P, 1], F32)
-        std = keep.tile([P, 1], F32)
+        root = keep.tile([P, 1], F32)
         rstd = keep.tile([P, 1], F32)
 
         def gain(first, end):
@@ -316,11 +330,11 @@ def tile_unified2dattentiononframe_pa_s_kernel(
             op0=ALU.mult, op1=ALU.subtract,
         )
         nc.scalar.activation(
-            out=std[:], in_=sum_sq[:, last + 1 : last + 2], func=ACT.Sqrt,
+            out=root[:], in_=sum_sq[:, last + 1 : last + 2], func=ACT.Abs_reciprocal_sqrt,
             bias=rest[:, 0:1], scale=1.0 / COLS,
         )
+        nc.scalar.activation(out=rstd[:], in_=root[:], func=ACT.Copy, scale=sign[:, 0:1])
         gain(PAIR, 2 * PAIR)
-        nc.vector.reciprocal(out=rstd[:], in_=std[:])
         gain(2 * PAIR, 2 * PAIR + HEAD)
         shift_and_store(0)
         gain(2 * PAIR + HEAD, 3 * PAIR)

@@ -27,13 +27,13 @@ BIAS_ROWS = CHANNELS // ROW_VALUES
 GAIN_ROWS = COLS // ROW_VALUES
 HEADS = 8
 HEAD = COLS // HEADS
+SIDE_PIECES = (256, 384, 384)
 PAIR = 2 * HEAD
 PAIRS = HEADS // 2
 ROWS_PER_PAIR = PAIR // ROW_VALUES
 RUN = 4
-WARM_PRODUCTS = 3
-WARM_COLS = 256
-KEEP_WARM_COLS = 64
+WARM_PRODUCTS = 4
+EARLY_TILES = 3
 T_AHEAD = 3
 Q_AHEAD = 2
 
@@ -48,8 +48,22 @@ def tile_unified2dattentiononframe_pa_s_kernel(
 
     with ExitStack() as stack:
         keep = stack.enter_context(tc.tile_pool(name="keep", bufs=1))
-        psum = stack.enter_context(tc.psum_pool(name="psum", bufs=8))
+        psum = stack.enter_context(tc.psum_pool(name="psum", bufs=7))
+        idle_psum = stack.enter_context(tc.psum_pool(name="idle_psum", bufs=1))
         stack.enter_context(tc.manual_schedule())
+
+        zeros = keep.tile([P, P], F32)
+        nc.vector.memset(zeros[:], 0.0)
+
+        idle_bank = idle_psum.tile([P, BANK], F32)
+
+        def idle_product(width):
+            nc.tensor.matmul(
+                idle_bank[:, 0:width], lhsT=zeros[:], rhs=zeros[:, 0:width], start=True, stop=True
+            )
+
+        for k in range(WARM_PRODUCTS):
+            idle_product(P)
 
         def load_columns(queue, vec, n_rows, label):
             columns = keep.tile([P, n_rows], F32, name=label)
@@ -106,18 +120,6 @@ def tile_unified2dattentiononframe_pa_s_kernel(
 
         bias_signed = signed_columns(bias_cols, BIAS_ROWS, "bias_signed")
 
-        zeros = keep.tile([P, WARM_COLS], F32)
-        nc.vector.memset(zeros[:], 0.0)
-
-        def idle_product(out):
-            nc.tensor.matmul(
-                out, lhsT=zeros[:, 0:P], rhs=zeros[:, 0 : out.shape[1]], start=True, stop=True
-            )
-
-        warm_ps = psum.tile([P, BANK], F32, tag="bank")
-        for k in range(WARM_PRODUCTS):
-            idle_product(warm_ps[:, 0:WARM_COLS])
-
         x_grouped = keep.tile([P, BANK, PACK], BF16, align_bytes=64)
         x_codes = keep.tile([P, BANK], U32, align_bytes=64)
         x_scales = keep.tile([P, BANK], U8, align_bytes=64)
@@ -148,13 +150,13 @@ def tile_unified2dattentiononframe_pa_s_kernel(
         w_scales = keep.tile([P, CHANNELS], U8, align_bytes=64)
 
         def transpose_w(j):
-            w_t = psum.tile([P, 4, P], F32, tag="bank")
+            w_t = psum.tile([P, 2, P], F32, tag="bank")
             for u in range(2):
                 words = w_words[:, j * (CIN // 2) + u : (j + 1) * (CIN // 2) : 2]
                 nc.tensor.transpose(w_t[:, u, :], words, ident[:])
-            idle_product(w_t[:, 2, 0:KEEP_WARM_COLS])
+            idle_product(P if j < EARLY_TILES else P // 2)
             nc.scalar.copy(
-                out=w_grouped_words[:, j, :, :], in_=w_t[:, 0:2, :].rearrange("q u o -> q o u")
+                out=w_grouped_words[:, j, :, :], in_=w_t[:].rearrange("q u o -> q o u")
             )
 
         def spread_rows(bank, columns, first_row, n_rows):
@@ -301,6 +303,26 @@ def tile_unified2dattentiononframe_pa_s_kernel(
                 op0=ALU.add, op1=ALU.mult,
             )
 
+        side_start = COLS - sum(SIDE_PIECES)
+        offsets = keep.tile([P, sum(SIDE_PIECES)], F32)
+        side_gamma = keep.tile([P, sum(SIDE_PIECES) // 2], F32)
+
+        def gain_beside(first, end):
+            side = slice(first - side_start, end - side_start)
+            pair = first // PAIR
+            nc.scalar.copy(
+                out=side_gamma[:, side.start // 2 : side.stop // 2],
+                in_=gamma_banks[pair][:, (first - pair * PAIR) // 2 : (end - pair * PAIR) // 2],
+            )
+            nc.scalar.activation(
+                out=offsets[:, side], in_=prelu[:, first:end],
+                func=ACT.Identity, bias=neg_mean[:, 0:1], scale=1.0,
+            )
+            nc.gpsimd.tensor_tensor(
+                out=centred[:, first:end], in0=offsets[:, side],
+                in1=side_gamma[:].bitcast(BF16)[:, side], op=ALU.mult,
+            )
+
         def shift_and_store(pair):
             cols = slice(pair * PAIR, (pair + 1) * PAIR)
             nc.vector.scalar_tensor_tensor(
@@ -324,7 +346,7 @@ def tile_unified2dattentiononframe_pa_s_kernel(
         nc.scalar.activation(
             out=offset_sq[:], in_=neg_mean[:], func=ACT.Square, bias=shift[:, 0:1], scale=1.0
         )
-        gain(0, PAIR)
+        gain(0, HEAD)
         nc.vector.scalar_tensor_tensor(
             out=rest[:], in0=early_sq[:], scalar=1.0 / COLS, in1=offset_sq[:],
             op0=ALU.mult, op1=ALU.subtract,
@@ -334,12 +356,13 @@ def tile_unified2dattentiononframe_pa_s_kernel(
             bias=rest[:, 0:1], scale=1.0 / COLS,
         )
         nc.scalar.activation(out=rstd[:], in_=root[:], func=ACT.Copy, scale=sign[:, 0:1])
+        first = side_start
+        for width in SIDE_PIECES:
+            gain_beside(first, first + width)
+            first += width
+        gain(HEAD, PAIR)
         gain(PAIR, 2 * PAIR)
-        gain(2 * PAIR, 2 * PAIR + HEAD)
         shift_and_store(0)
-        gain(2 * PAIR + HEAD, 3 * PAIR)
-        shift_and_store(1)
-        gain(3 * PAIR, 3 * PAIR + HEAD)
-        shift_and_store(2)
-        gain(3 * PAIR + HEAD, 4 * PAIR)
-        shift_and_store(3)
+        gain(2 * PAIR, side_start)
+        for pair in range(1, PAIRS):
+            shift_and_store(pair)

@@ -27,7 +27,7 @@ BIAS_ROWS = CHANNELS // ROW_VALUES
 GAIN_ROWS = COLS // ROW_VALUES
 HEADS = 8
 HEAD = COLS // HEADS
-SIDE_PIECES = (256, 384, 384)
+SIDE_HEADS = (2, 4, 6)
 PAIR = 2 * HEAD
 PAIRS = HEADS // 2
 ROWS_PER_PAIR = PAIR // ROW_VALUES
@@ -154,7 +154,8 @@ def tile_unified2dattentiononframe_pa_s_kernel(
             for u in range(2):
                 words = w_words[:, j * (CIN // 2) + u : (j + 1) * (CIN // 2) : 2]
                 nc.tensor.transpose(w_t[:, u, :], words, ident[:])
-            idle_product(P if j < EARLY_TILES else P // 2)
+            if j >= EARLY_TILES:
+                idle_product(P // 2)
             nc.scalar.copy(
                 out=w_grouped_words[:, j, :, :], in_=w_t[:].rearrange("q u o -> q o u")
             )
@@ -180,8 +181,12 @@ def tile_unified2dattentiononframe_pa_s_kernel(
         y = keep.tile([P, COLS], F32)
         prelu = keep.tile([P, COLS], F32)
         squares = keep.tile([P, COLS], F32)
-        sum_p = keep.tile([P, O_TILES], F32)
-        sum_sq = keep.tile([P, O_TILES + 1], F32)
+        pieces = [(j * BANK, (j + 1) * BANK) for j in range(O_TILES - 1)]
+        pieces.append((COLS - BANK, COLS - BANK // 2))
+        pieces.append((COLS - BANK // 2, COLS))
+        n_pieces = len(pieces)
+        sum_p = keep.tile([P, n_pieces], F32)
+        sum_sq = keep.tile([P, n_pieces + 1], F32)
         nc.vector.tensor_scalar(
             out=sum_sq[:, 0:1], in0=one[:], scalar1=COLS * EPS, scalar2=0.0,
             op0=ALU.mult, op1=ALU.add,
@@ -215,13 +220,13 @@ def tile_unified2dattentiononframe_pa_s_kernel(
                 op0=ALU.mult, op1=ALU.add,
             )
 
-        def activate(j):
-            cols = slice(j * BANK, (j + 1) * BANK)
+        def activate(i):
+            cols = slice(*pieces[i])
             nc.vector.scalar_tensor_tensor(
                 out=prelu[:, cols], in0=y[:, cols], scalar=alpha_bc[:, 0:1],
-                in1=y[:, cols], op0=ALU.mult, op1=ALU.max, accum_out=sum_p[:, j : j + 1],
+                in1=y[:, cols], op0=ALU.mult, op1=ALU.max, accum_out=sum_p[:, i : i + 1],
             )
-            if j == 0:
+            if i == 0:
                 nc.scalar.activation(
                     out=neg_shift[:], in_=sum_p[:, 0:1], func=ACT.Copy, scale=-1.0 / BANK,
                 )
@@ -229,22 +234,25 @@ def tile_unified2dattentiononframe_pa_s_kernel(
                     out=shift[:], in_=sum_p[:, 0:1], func=ACT.Copy, scale=1.0 / BANK,
                 )
 
-        def square(j):
-            cols = slice(j * BANK, (j + 1) * BANK)
+        def square(i):
+            cols = slice(*pieces[i])
             nc.scalar.activation(
                 out=squares[:, cols], in_=prelu[:, cols], func=ACT.Square,
-                bias=neg_shift[:, 0:1], scale=1.0, accum_out=sum_sq[:, j + 1 : j + 2],
+                bias=neg_shift[:, 0:1], scale=1.0, accum_out=sum_sq[:, i + 1 : i + 2],
             )
 
         group_x(0)
         group_x(1)
-        for j in range(T_AHEAD - 1):
+        for j in range(T_AHEAD):
             transpose_w(j)
             if j == 0:
+                idle_product(P)
+                idle_product(P)
                 group_x(FREQ - 1)
                 bias_ps = psum.tile([P, BANK], F32, tag="bank")
                 spread_rows(bias_ps, bias_signed, 0, BIAS_ROWS)
                 nc.scalar.copy(out=bias_words[:], in_=bias_ps[:, 0 : BIAS_ROWS * P])
+                idle_product(P)
         quantise_w(0)
         group_x(2)
         quantise_x(0)
@@ -253,9 +261,9 @@ def tile_unified2dattentiononframe_pa_s_kernel(
         gamma_banks = []
         beta_banks = []
 
-        def spread_gain_and_shift():
+        def spread_gain_and_shift(gamma_signed):
             for banks, columns, label in (
-                (gamma_banks, gamma_cols, "gamma"),
+                (gamma_banks, gamma_signed, "gamma"),
                 (beta_banks, beta_cols, "beta"),
             ):
                 for k in range(PAIRS):
@@ -263,35 +271,46 @@ def tile_unified2dattentiononframe_pa_s_kernel(
                     spread_rows(bank, columns, k * ROWS_PER_PAIR, ROWS_PER_PAIR)
                     banks.append(bank[:, 0 : PAIR // 2])
 
-        for s in range(O_TILES + 2):
+        side_gamma = keep.tile([P, len(SIDE_HEADS) * HEAD // 2], F32)
+
+        def copy_side_gamma(k):
+            pair, second = divmod(SIDE_HEADS[k], 2)
+            words = HEAD // 2
+            nc.scalar.copy(
+                out=side_gamma[:, k * words : (k + 1) * words],
+                in_=gamma_banks[pair][:, second * words : (second + 1) * words],
+            )
+
+        for s in range(O_TILES):
+            if s == O_TILES - 2:
+                gamma_signed = signed_columns(gamma_cols, GAIN_ROWS, "gamma_signed")
             if s < O_TILES:
                 multiply(s)
-            if s == 0:
-                transpose_w(T_AHEAD - 1)
             if s + T_AHEAD < O_TILES:
                 transpose_w(s + T_AHEAD)
             if s == O_TILES - 1:
-                spread_gain_and_shift()
+                spread_gain_and_shift(gamma_signed)
             if s < O_TILES:
                 add_bias(s)
             if s + Q_AHEAD < O_TILES:
                 quantise_w(s + Q_AHEAD)
-            if s == O_TILES:
-                nc.vector.tensor_reduce(
-                    out=early_p[:], in_=sum_p[:, 0 : O_TILES - 1], axis=AXIS.X, op=ALU.add
-                )
-            if 1 <= s < O_TILES + 1:
+            if 1 <= s < O_TILES:
                 activate(s - 1)
-            if s >= 2:
+            if 2 <= s < O_TILES:
                 square(s - 2)
+        activate(O_TILES - 1)
+        activate(O_TILES)
+        copy_side_gamma(0)
+        square(O_TILES - 2)
+        square(O_TILES - 1)
+        square(O_TILES)
 
         centred = keep.tile([P, COLS], F32)
         result = keep.tile([P, COLS], F32)
         neg_mean = keep.tile([P, 1], F32)
         offset_sq = keep.tile([P, 1], F32)
-        early_sq = keep.tile([P, 1], F32)
-        rest = keep.tile([P, 1], F32)
-        root = keep.tile([P, 1], F32)
+        mean_sq = keep.tile([P, 1], F32)
+        scaled_sq = keep.tile([P, n_pieces + 1], F32)
         rstd = keep.tile([P, 1], F32)
 
         def gain(first, end):
@@ -303,66 +322,76 @@ def tile_unified2dattentiononframe_pa_s_kernel(
                 op0=ALU.add, op1=ALU.mult,
             )
 
-        side_start = COLS - sum(SIDE_PIECES)
-        offsets = keep.tile([P, sum(SIDE_PIECES)], F32)
-        side_gamma = keep.tile([P, sum(SIDE_PIECES) // 2], F32)
+        offsets = keep.tile([P, len(SIDE_HEADS) * HEAD], F32)
 
-        def gain_beside(first, end):
-            side = slice(first - side_start, end - side_start)
-            pair = first // PAIR
-            nc.scalar.copy(
-                out=side_gamma[:, side.start // 2 : side.stop // 2],
-                in_=gamma_banks[pair][:, (first - pair * PAIR) // 2 : (end - pair * PAIR) // 2],
-            )
+        def gain_beside(k):
+            cols = slice(SIDE_HEADS[k] * HEAD, (SIDE_HEADS[k] + 1) * HEAD)
+            side = slice(k * HEAD, (k + 1) * HEAD)
             nc.scalar.activation(
-                out=offsets[:, side], in_=prelu[:, first:end],
+                out=offsets[:, side], in_=prelu[:, cols],
                 func=ACT.Identity, bias=neg_mean[:, 0:1], scale=1.0,
             )
             nc.gpsimd.tensor_tensor(
-                out=centred[:, first:end], in0=offsets[:, side],
+                out=centred[:, cols], in0=offsets[:, side],
                 in1=side_gamma[:].bitcast(BF16)[:, side], op=ALU.mult,
             )
 
-        def shift_and_store(pair):
-            cols = slice(pair * PAIR, (pair + 1) * PAIR)
+        def add_shift(head):
+            first, end = head * HEAD, (head + 1) * HEAD
+            pair = head // 2
+            words = beta_banks[pair].bitcast(BF16)
             nc.vector.scalar_tensor_tensor(
-                out=result[:, cols], in0=centred[:, cols], scalar=rstd[:, 0:1],
-                in1=beta_banks[pair].bitcast(BF16), op0=ALU.mult, op1=ALU.add,
+                out=result[:, first:end], in0=centred[:, first:end], scalar=rstd[:, 0:1],
+                in1=words[:, first - pair * PAIR : end - pair * PAIR],
+                op0=ALU.mult, op1=ALU.add,
             )
-            by_kind = result[:, cols].rearrange("t (h k d) -> t k h d", h=2, k=3)
-            for k in range(3):
-                nc.sync.dma_start(
-                    out=out_views[k][:, 2 * pair : 2 * pair + 2, :], in_=by_kind[:, k, :, :]
-                )
 
-        last = O_TILES - 1
+        by_kind = result[:].rearrange("t (h k d) -> t k h d", h=HEADS, k=3)
+
+        def store(pair):
+            heads = slice(2 * pair, 2 * pair + 2)
+            for kind in range(3):
+                nc.sync.dma_start(out=out_views[kind][:, heads, :], in_=by_kind[:, kind, heads, :])
+
+        def gain_head(head):
+            gain(head * HEAD, (head + 1) * HEAD)
+
+        last = n_pieces - 1
+        nc.vector.tensor_reduce(out=early_p[:], in_=sum_p[:, 0:last], axis=AXIS.X, op=ALU.add)
         nc.vector.tensor_scalar(
             out=neg_mean[:], in0=sum_p[:, last : last + 1], scalar1=early_p[:, 0:1],
             scalar2=-1.0 / COLS, op0=ALU.add, op1=ALU.mult,
         )
-        nc.vector.tensor_reduce(
-            out=early_sq[:], in_=sum_sq[:, 0 : last + 1], axis=AXIS.X, op=ALU.add
-        )
         nc.scalar.activation(
             out=offset_sq[:], in_=neg_mean[:], func=ACT.Square, bias=shift[:, 0:1], scale=1.0
         )
-        gain(0, HEAD)
-        nc.vector.scalar_tensor_tensor(
-            out=rest[:], in0=early_sq[:], scalar=1.0 / COLS, in1=offset_sq[:],
-            op0=ALU.mult, op1=ALU.subtract,
-        )
         nc.scalar.activation(
-            out=root[:], in_=sum_sq[:, last + 1 : last + 2], func=ACT.Abs_reciprocal_sqrt,
-            bias=rest[:, 0:1], scale=1.0 / COLS,
+            out=scaled_sq[:], in_=sum_sq[:], func=ACT.Identity, scale=1.0 / COLS,
+            accum_out=mean_sq[:],
         )
-        nc.scalar.activation(out=rstd[:], in_=root[:], func=ACT.Copy, scale=sign[:, 0:1])
-        first = side_start
-        for width in SIDE_PIECES:
-            gain_beside(first, first + width)
-            first += width
-        gain(HEAD, PAIR)
-        gain(PAIR, 2 * PAIR)
-        shift_and_store(0)
-        gain(2 * PAIR, side_start)
-        for pair in range(1, PAIRS):
-            shift_and_store(pair)
+        gain_head(0)
+        gain_head(1)
+        nc.scalar.activation(
+            out=rstd[:], in_=offset_sq[:], func=ACT.Abs_reciprocal_sqrt,
+            bias=mean_sq[:, 0:1], scale=-1.0,
+        )
+        gain_beside(0)
+        copy_side_gamma(1)
+        gain_beside(1)
+        copy_side_gamma(2)
+        gain_beside(2)
+        gain_head(3)
+        add_shift(0)
+        add_shift(1)
+        store(0)
+        gain_head(5)
+        add_shift(2)
+        add_shift(3)
+        store(1)
+        gain_head(7)
+        add_shift(4)
+        add_shift(5)
+        store(2)
+        add_shift(6)
+        add_shift(7)
+        store(3)

@@ -34,8 +34,8 @@ ROWS_PER_PAIR = PAIR // ROW_VALUES
 RUN = 4
 WARM_PRODUCTS = 4
 EARLY_TILES = 3
+TURNED = 2
 T_AHEAD = 3
-Q_AHEAD = 2
 
 FLOPS = 2 * CHANNELS * CIN * FREQ * P
 
@@ -87,6 +87,11 @@ def tile_unified2dattentiononframe_pa_s_kernel(
         for j in range(1, O_TILES):
             nc.sync.dma_start(out=w_raw[:, j, :], in_=w_rows[:, j, :])
 
+        turned_bias = keep.tile([P, 1], BF16)
+        nc.sync.dma_start(
+            out=turned_bias[:],
+            in_=qkv_b[TURNED * P : (TURNED + 1) * P].rearrange("(r e) -> r e", e=1),
+        )
         gamma_cols = load_columns(
             nc.sync, qkv_gamma.rearrange("a o b f -> (a o b f)"), GAIN_ROWS, "gamma_cols"
         )
@@ -258,6 +263,7 @@ def tile_unified2dattentiononframe_pa_s_kernel(
         quantise_x(0)
         quantise_x(1)
         quantise_w(1)
+
         gamma_banks = []
         beta_banks = []
 
@@ -281,29 +287,85 @@ def tile_unified2dattentiononframe_pa_s_kernel(
                 in_=gamma_banks[pair][:, second * words : (second + 1) * words],
             )
 
-        for s in range(O_TILES):
-            if s == O_TILES - 2:
-                gamma_signed = signed_columns(gamma_cols, GAIN_ROWS, "gamma_signed")
-            if s < O_TILES:
-                multiply(s)
-            if s + T_AHEAD < O_TILES:
-                transpose_w(s + T_AHEAD)
-            if s == O_TILES - 1:
-                spread_gain_and_shift(gamma_signed)
-            if s < O_TILES:
-                add_bias(s)
-            if s + Q_AHEAD < O_TILES:
-                quantise_w(s + Q_AHEAD)
-            if 1 <= s < O_TILES:
-                activate(s - 1)
-            if 2 <= s < O_TILES:
-                square(s - 2)
-        activate(O_TILES - 1)
-        activate(O_TILES)
+        turned_y = keep.tile([P, BANK], F32)
+        turned_signed = keep.tile([P, 1], F32)
+
+        def multiply_turned():
+            j = TURNED
+            z = psum.tile([P, BANK], F32, tag="bank")
+            nc.tensor.matmul_mx(
+                out=z[:],
+                lhsT=w_codes[:, j * P : (j + 1) * P].bitcast(FP8X4),
+                lhsT_scale=w_scales[:, j * P : (j + 1) * P],
+                rhs=x_codes[:].bitcast(FP8X4), rhs_scale=x_scales[:],
+                start=True, stop=True,
+            )
+            nc.scalar.activation(
+                out=turned_y[:], in_=z[:], func=ACT.Identity,
+                bias=turned_signed[:, 0:1], scale=sign[:, 0:1],
+            )
+
+        def turn():
+            y_t = psum.tile([P, FREQ, P], F32, tag="bank")
+            for f in range(FREQ):
+                nc.tensor.transpose(y_t[:, f, :], turned_y[:, f * P : (f + 1) * P], ident[:])
+            products[TURNED] = y_t
+
+        def copy_turned():
+            nc.scalar.copy(
+                out=y[:, TURNED * BANK : (TURNED + 1) * BANK].rearrange("t (o f) -> t o f", f=FREQ),
+                in_=products[TURNED][:].rearrange("t f o -> t o f"),
+            )
+
+        def activate_turned():
+            cols = slice(*pieces[TURNED])
+            nc.vector.scalar_tensor_tensor(
+                out=prelu[:, cols].rearrange("t (o f) -> t o f", f=FREQ),
+                in0=products[TURNED][:].rearrange("t f o -> t o f"), scalar=alpha_bc[:, 0:1],
+                in1=y[:, cols].rearrange("t (o f) -> t o f", f=FREQ),
+                op0=ALU.mult, op1=ALU.max, accum_out=sum_p[:, TURNED : TURNED + 1],
+            )
+
+        multiply(0)
+        transpose_w(3)
+        add_bias(0)
+        quantise_w(2)
+        multiply(1)
+        transpose_w(4)
+        nc.scalar.activation(
+            out=turned_signed[:], in_=turned_bias[:], func=ACT.Copy, scale=sign[:, 0:1]
+        )
+        multiply_turned()
+        add_bias(1)
+        quantise_w(3)
+        activate(0)
+        multiply(3)
+        transpose_w(5)
+        quantise_w(4)
+        activate(1)
+        turn()
+        copy_turned()
+        add_bias(3)
+        square(0)
+        multiply(4)
+        quantise_w(5)
+        activate(3)
+        square(1)
+        gamma_signed = signed_columns(gamma_cols, GAIN_ROWS, "gamma_signed")
+        activate_turned()
+        add_bias(4)
+        multiply(5)
+        spread_gain_and_shift(gamma_signed)
+        square(3)
+        square(2)
         copy_side_gamma(0)
-        square(O_TILES - 2)
-        square(O_TILES - 1)
-        square(O_TILES)
+        add_bias(5)
+        activate(4)
+        square(4)
+        activate(5)
+        activate(6)
+        square(5)
+        square(6)
 
         centred = keep.tile([P, COLS], F32)
         result = keep.tile([P, COLS], F32)
@@ -327,10 +389,16 @@ def tile_unified2dattentiononframe_pa_s_kernel(
         def gain_beside(k):
             cols = slice(SIDE_HEADS[k] * HEAD, (SIDE_HEADS[k] + 1) * HEAD)
             side = slice(k * HEAD, (k + 1) * HEAD)
-            nc.scalar.activation(
-                out=offsets[:, side], in_=prelu[:, cols],
-                func=ACT.Identity, bias=neg_mean[:, 0:1], scale=1.0,
-            )
+            if k == 0:
+                nc.gpsimd.tensor_scalar(
+                    out=offsets[:, side], in0=prelu[:, cols], scalar1=neg_mean[:, 0:1],
+                    scalar2=1.0, op0=ALU.add, op1=ALU.mult,
+                )
+            else:
+                nc.scalar.activation(
+                    out=offsets[:, side], in_=prelu[:, cols],
+                    func=ACT.Identity, bias=neg_mean[:, 0:1], scale=1.0,
+                )
             nc.gpsimd.tensor_tensor(
                 out=centred[:, cols], in0=offsets[:, side],
                 in1=side_gamma[:].bitcast(BF16)[:, side], op=ALU.mult,
@@ -380,18 +448,18 @@ def tile_unified2dattentiononframe_pa_s_kernel(
         gain_beside(1)
         copy_side_gamma(2)
         gain_beside(2)
-        gain_head(3)
         add_shift(0)
         add_shift(1)
         store(0)
-        gain_head(5)
+        gain_head(3)
         add_shift(2)
         add_shift(3)
         store(1)
-        gain_head(7)
+        gain_head(5)
         add_shift(4)
         add_shift(5)
         store(2)
+        gain_head(7)
         add_shift(6)
         add_shift(7)
         store(3)

@@ -27,7 +27,7 @@ BIAS_ROWS = CHANNELS // ROW_VALUES
 GAIN_ROWS = COLS // ROW_VALUES
 HEADS = 8
 HEAD = COLS // HEADS
-SIDE_HEADS = (2, 4, 6)
+SIDE_HEADS = (2, 4, 6, 7)
 PAIR = 2 * HEAD
 PAIRS = HEADS // 2
 ROWS_PER_PAIR = PAIR // ROW_VALUES
@@ -77,14 +77,13 @@ def tile_unified2dattentiononframe_pa_s_kernel(
         nc.scalar.dma_start(out=alpha_bc[:], in_=qkv_alpha.partition_broadcast(P))
         bias_cols = load_columns(nc.scalar, qkv_b, BIAS_ROWS, "bias_cols")
         x_raw = keep.tile([P, PACK, BANK], BF16)
-        x_rows = x.rearrange("a (q s) f t -> q (a s) (f t)", s=PACK)
         w_raw = keep.tile([P, O_TILES, CIN], BF16)
         w_rows = qkv_w.rearrange("(j r) c -> r j c", r=P)
-        nc.sync.dma_start(out=w_raw[:, 0, :], in_=w_rows[:, 0, :])
-        for half in range(2):
-            cols = slice(half * BANK // 2, (half + 1) * BANK // 2)
-            nc.sync.dma_start(out=x_raw[:, :, cols], in_=x_rows[:, :, cols])
-        for j in range(1, O_TILES):
+        nc.sync.dma_start(
+            out=x_raw[:].rearrange("q s w -> q (s w)"),
+            in_=x.rearrange("a (q s) f t -> q (a s f t)", s=PACK),
+        )
+        for j in range(O_TILES):
             nc.sync.dma_start(out=w_raw[:, j, :], in_=w_rows[:, j, :])
 
         turned_bias = keep.tile([P, 1], BF16)
@@ -186,9 +185,8 @@ def tile_unified2dattentiononframe_pa_s_kernel(
         y = keep.tile([P, COLS], F32)
         prelu = keep.tile([P, COLS], F32)
         squares = keep.tile([P, COLS], F32)
-        pieces = [(j * BANK, (j + 1) * BANK) for j in range(O_TILES - 1)]
-        pieces.append((COLS - BANK, COLS - BANK // 2))
-        pieces.append((COLS - BANK // 2, COLS))
+        pieces = [(j * BANK, (j + 1) * BANK) for j in range(O_TILES - 2)]
+        pieces += [(h * BANK // 2, (h + 1) * BANK // 2) for h in range(2 * O_TILES - 4, 2 * O_TILES)]
         n_pieces = len(pieces)
         sum_p = keep.tile([P, n_pieces], F32)
         sum_sq = keep.tile([P, n_pieces + 1], F32)
@@ -246,22 +244,19 @@ def tile_unified2dattentiononframe_pa_s_kernel(
                 bias=neg_shift[:, 0:1], scale=1.0, accum_out=sum_sq[:, i + 1 : i + 2],
             )
 
-        group_x(0)
-        group_x(1)
+        for f in range(FREQ):
+            group_x(f)
         for j in range(T_AHEAD):
             transpose_w(j)
             if j == 0:
                 idle_product(P)
-                idle_product(P)
-                group_x(FREQ - 1)
                 bias_ps = psum.tile([P, BANK], F32, tag="bank")
                 spread_rows(bias_ps, bias_signed, 0, BIAS_ROWS)
                 nc.scalar.copy(out=bias_words[:], in_=bias_ps[:, 0 : BIAS_ROWS * P])
                 idle_product(P)
-        quantise_w(0)
-        group_x(2)
         quantise_x(0)
         quantise_x(1)
+        quantise_w(0)
         quantise_w(1)
 
         gamma_banks = []
@@ -347,25 +342,21 @@ def tile_unified2dattentiononframe_pa_s_kernel(
         copy_turned()
         add_bias(3)
         square(0)
+        gamma_signed = signed_columns(gamma_cols, GAIN_ROWS, "gamma_signed")
         multiply(4)
         quantise_w(5)
         activate(3)
         square(1)
-        gamma_signed = signed_columns(gamma_cols, GAIN_ROWS, "gamma_signed")
         activate_turned()
         add_bias(4)
         multiply(5)
         spread_gain_and_shift(gamma_signed)
         square(3)
         square(2)
-        copy_side_gamma(0)
         add_bias(5)
-        activate(4)
-        square(4)
-        activate(5)
-        activate(6)
-        square(5)
-        square(6)
+        for i in range(O_TILES - 2, n_pieces):
+            activate(i)
+            square(i)
 
         centred = keep.tile([P, COLS], F32)
         result = keep.tile([P, COLS], F32)
@@ -433,6 +424,7 @@ def tile_unified2dattentiononframe_pa_s_kernel(
         nc.scalar.activation(
             out=offset_sq[:], in_=neg_mean[:], func=ACT.Square, bias=shift[:, 0:1], scale=1.0
         )
+        copy_side_gamma(0)
         nc.scalar.activation(
             out=scaled_sq[:], in_=sum_sq[:], func=ACT.Identity, scale=1.0 / COLS,
             accum_out=mean_sq[:],
@@ -448,6 +440,8 @@ def tile_unified2dattentiononframe_pa_s_kernel(
         gain_beside(1)
         copy_side_gamma(2)
         gain_beside(2)
+        copy_side_gamma(3)
+        gain_beside(3)
         add_shift(0)
         add_shift(1)
         store(0)
@@ -459,7 +453,6 @@ def tile_unified2dattentiononframe_pa_s_kernel(
         add_shift(4)
         add_shift(5)
         store(2)
-        gain_head(7)
         add_shift(6)
         add_shift(7)
         store(3)

from contextlib import ExitStack

import concourse.mybir as mybir
from concourse.masks import make_identity

F32 = mybir.dt.float32
BF16 = mybir.dt.bfloat16
U32 = mybir.dt.uint32
U8 = mybir.dt.uint8
FP8X4 = mybir.dt.float8_e4m3fn_x4
ALU = mybir.AluOpType
ACT = mybir.ActivationFunctionType
AXIS = mybir.AxisListType

P = 128
PACK = 4
CIN = P * PACK
FREQ = 4
CHANNELS = 768
O_TILES = CHANNELS // P
BANK = P * FREQ
COLS = CHANNELS * FREQ
HEAD_DIM = 128
EPS = 1e-5
ROW_VALUES = 2 * P
BIAS_ROWS = CHANNELS // ROW_VALUES
GAIN_ROWS = COLS // ROW_VALUES
HEADS = 8
HEAD = COLS // HEADS
SIDE_HEADS = (2, 4, 6, 7)
PAIR = 2 * HEAD
PAIRS = HEADS // 2
ROWS_PER_PAIR = PAIR // ROW_VALUES
RUN = 4
WARM_PRODUCTS = 4
EARLY_TILES = 3
TURNED = 2
T_AHEAD = 3

FLOPS = 2 * CHANNELS * CIN * FREQ * P


def tile_unified2dattentiononframe_pa_s_kernel(
    tc, x, qkv_w, qkv_b, qkv_alpha, qkv_gamma, qkv_beta, out_0, out_1, out_2
):
    nc = tc.nc
    out_views = [o.rearrange("a h t d -> t (a h) d") for o in (out_0, out_1, out_2)]

    with ExitStack() as stack:
        keep = stack.enter_context(tc.tile_pool(name="keep", bufs=1))
        psum = stack.enter_context(tc.psum_pool(name="psum", bufs=7))
        idle_psum = stack.enter_context(tc.psum_pool(name="idle_psum", bufs=1))
        stack.enter_context(tc.manual_schedule())

        zeros = keep.tile([P, P], F32)
        nc.vector.memset(zeros[:], 0.0)

        idle_bank = idle_psum.tile([P, BANK], F32)

        def idle_product(width):
            nc.tensor.matmul(
                idle_bank[:, 0:width], lhsT=zeros[:], rhs=zeros[:, 0:width], start=True, stop=True
            )

        for k in range(WARM_PRODUCTS):
            idle_product(P)

        def load_columns(queue, vec, n_rows, label):
            columns = keep.tile([P, n_rows], F32, name=label)
            queue.dma_start(
                out=columns[:].bitcast(BF16).rearrange("w (r e) -> w r e", e=2),
                in_=vec.rearrange("(r w e) -> w r e", w=P, e=2),
            )
            return columns

        alpha_bc = keep.tile([P, 1], BF16)
        nc.scalar.dma_start(out=alpha_bc[:], in_=qkv_alpha.partition_broadcast(P))
        bias_cols = load_columns(nc.scalar, qkv_b, BIAS_ROWS, "bias_cols")
        x_raw = keep.tile([P, PACK, BANK], BF16)
        w_raw = keep.tile([P, O_TILES, CIN], BF16)
        w_rows = qkv_w.rearrange("(j r) c -> r j c", r=P)
        nc.sync.dma_start(
            out=x_raw[:].rearrange("q s w -> q (s w)"),
            in_=x.rearrange("a (q s) f t -> q (a s f t)", s=PACK),
        )
        for j in range(O_TILES):
            nc.sync.dma_start(out=w_raw[:, j, :], in_=w_rows[:, j, :])

        turned_bias = keep.tile([P, 1], BF16)
        nc.sync.dma_start(
            out=turned_bias[:],
            in_=qkv_b[TURNED * P : (TURNED + 1) * P].rearrange("(r e) -> r e", e=1),
        )
        gamma_cols = load_columns(
            nc.sync, qkv_gamma.rearrange("a o b f -> (a o b f)"), GAIN_ROWS, "gamma_cols"
        )
        beta_cols = load_columns(
            nc.sync, qkv_beta.rearrange("a o b f -> (a o b f)"), GAIN_ROWS, "beta_cols"
        )

        ident = keep.tile([P, P], F32)
        make_identity(nc, ident[:])
        one = keep.tile([P, 1], F32)
        nc.vector.memset(one[:], 1.0)
        warm = keep.tile([P, 1], F32)
        nc.scalar.activation(out=warm[:], in_=one[:], func=ACT.Abs_reciprocal_sqrt)

        sign = keep.tile([P, 1], F32)
        one_plus = keep.tile([P, 1], F32)
        nc.vector.tensor_scalar(
            out=one_plus[:], in0=one[:], scalar1=1.001, scalar2=0.0, op0=ALU.mult, op1=ALU.add
        )
        nc.scalar.activation(
            out=sign[:], in_=alpha_bc[:], func=ACT.Sign, bias=one_plus[:, 0:1], scale=-1.0
        )

        def signed_columns(columns, n_rows, label):
            signed = keep.tile([P, n_rows], F32, name=label)
            nc.scalar.activation(
                out=signed[:].bitcast(BF16), in_=columns[:].bitcast(BF16), func=ACT.Copy,
                scale=sign[:, 0:1],
            )
            return signed

        bias_signed = signed_columns(bias_cols, BIAS_ROWS, "bias_signed")

        x_grouped = keep.tile([P, BANK, PACK], BF16, align_bytes=64)
        x_codes = keep.tile([P, BANK], U32, align_bytes=64)
        x_scales = keep.tile([P, BANK], U8, align_bytes=64)

        def group_x(f):
            cols = slice(f * P, (f + 1) * P)
            dst = x_grouped[:, cols, :].rearrange("q (c i) s -> q c s i", i=RUN)
            src = x_raw[:, :, cols].rearrange("q s (c i) -> q c s i", i=RUN)
            if f < FREQ - 1:
                nc.vector.tensor_copy(out=dst, in_=src)
            else:
                nc.scalar.copy(out=dst, in_=src)

        def quantise_x(half):
            cols = slice(half * BANK // 2, (half + 1) * BANK // 2)
            nc.vector.quantize_mx(
                out=x_codes[:, cols].bitcast(FP8X4),
                scales=x_scales[:, cols],
                in_=x_grouped[:, cols, :].rearrange("q w s -> q (w s)"),
            )

        w_words = w_raw[:].rearrange("r j c -> r (j c)").bitcast(F32)
        w_grouped = keep.tile([P, CHANNELS * PACK], BF16, align_bytes=64)
        w_grouped_words = w_grouped[:].bitcast(F32).rearrange(
            "q (j o u) -> q j o u", j=O_TILES, u=2
        )
        w_codes = keep.tile([P, CHANNELS], U32, align_bytes=64)
        w_scales = keep.tile([P, CHANNELS], U8, align_bytes=64)

        def transpose_w(j):
            w_t = psum.tile([P, 2, P], F32, tag="bank")
            for u in range(2):
                words = w_words[:, j * (CIN // 2) + u : (j + 1) * (CIN // 2) : 2]
                nc.tensor.transpose(w_t[:, u, :], words, ident[:])
            if j >= EARLY_TILES:
                idle_product(P // 2)
            nc.scalar.copy(
                out=w_grouped_words[:, j, :, :], in_=w_t[:].rearrange("q u o -> q o u")
            )

        def spread_rows(bank, columns, first_row, n_rows):
            for r in range(n_rows):
                nc.tensor.transpose(
                    bank[:, r * P : (r + 1) * P],
                    columns[:, first_row + r : first_row + r + 1].to_broadcast([P, P]),
                    ident[:],
                )

        bias_words = keep.tile([P, BIAS_ROWS * P], F32)
        bias_bc = bias_words[:].bitcast(BF16)

        def quantise_w(j):
            nc.vector.quantize_mx(
                out=w_codes[:, j * P : (j + 1) * P].bitcast(FP8X4),
                scales=w_scales[:, j * P : (j + 1) * P],
                in_=w_grouped[:, j * BANK : (j + 1) * BANK],
            )

        y = keep.tile([P, COLS], F32)
        prelu = keep.tile([P, COLS], F32)
        squares = keep.tile([P, COLS], F32)
        pieces = [(j * BANK, (j + 1) * BANK) for j in range(O_TILES - 2)]
        pieces += [(h * BANK // 2, (h + 1) * BANK // 2) for h in range(2 * O_TILES - 4, 2 * O_TILES)]
        n_pieces = len(pieces)
        sum_p = keep.tile([P, n_pieces], F32)
        sum_sq = keep.tile([P, n_pieces + 1], F32)
        nc.vector.tensor_scalar(
            out=sum_sq[:, 0:1], in0=one[:], scalar1=COLS * EPS, scalar2=0.0,
            op0=ALU.mult, op1=ALU.add,
        )
        neg_shift = keep.tile([P, 1], F32)
        shift = keep.tile([P, 1], F32)
        early_p = keep.tile([P, 1], F32)

        products = {}

        def multiply(j):
            z = psum.tile([P, FREQ, P], F32, tag="bank")
            for f in range(FREQ):
                nc.tensor.matmul_mx(
                    out=z[:, f, :],
                    lhsT=x_codes[:, f * P : (f + 1) * P].bitcast(FP8X4),
                    lhsT_scale=x_scales[:, f * P : (f + 1) * P],
                    rhs=w_codes[:, j * P : (j + 1) * P].bitcast(FP8X4),
                    rhs_scale=w_scales[:, j * P : (j + 1) * P],
                    start=True,
                    stop=True,
                )
            products[j] = z

        def add_bias(j):
            cols = slice(j * BANK, (j + 1) * BANK)
            nc.vector.scalar_tensor_tensor(
                out=y[:, cols].rearrange("t (o f) -> t o f", f=FREQ),
                in0=products[j][:].rearrange("t f o -> t o f"), scalar=sign[:, 0:1],
                in1=bias_bc[:, j * P : (j + 1) * P].unsqueeze(2).to_broadcast([P, P, FREQ]),
                op0=ALU.mult, op1=ALU.add,
            )

        def activate(i):
            cols = slice(*pieces[i])
            nc.vector.scalar_tensor_tensor(
                out=prelu[:, cols], in0=y[:, cols], scalar=alpha_bc[:, 0:1],
                in1=y[:, cols], op0=ALU.mult, op1=ALU.max, accum_out=sum_p[:, i : i + 1],
            )
            if i == 0:
                nc.scalar.activation(
                    out=neg_shift[:], in_=sum_p[:, 0:1], func=ACT.Copy, scale=-1.0 / BANK,
                )
                nc.scalar.activation(
                    out=shift[:], in_=sum_p[:, 0:1], func=ACT.Copy, scale=1.0 / BANK,
                )

        def square(i):
            cols = slice(*pieces[i])
            nc.scalar.activation(
                out=squares[:, cols], in_=prelu[:, cols], func=ACT.Square,
                bias=neg_shift[:, 0:1], scale=1.0, accum_out=sum_sq[:, i + 1 : i + 2],
            )

        for f in range(FREQ):
            group_x(f)
        for j in range(T_AHEAD):
            transpose_w(j)
            if j == 0:
                idle_product(P)
                bias_ps = psum.tile([P, BANK], F32, tag="bank")
                spread_rows(bias_ps, bias_signed, 0, BIAS_ROWS)
                nc.scalar.copy(out=bias_words[:], in_=bias_ps[:, 0 : BIAS_ROWS * P])
                idle_product(P)
        quantise_x(0)
        quantise_x(1)
        quantise_w(0)
        quantise_w(1)

        gamma_banks = []
        beta_banks = []

        def spread_gain_and_shift(gamma_signed):
            for banks, columns, label in (
                (gamma_banks, gamma_signed, "gamma"),
                (beta_banks, beta_cols, "beta"),
            ):
                for k in range(PAIRS):
                    bank = psum.tile([P, BANK], F32, tag="bank", name="%s%d" % (label, k))
                    spread_rows(bank, columns, k * ROWS_PER_PAIR, ROWS_PER_PAIR)
                    banks.append(bank[:, 0 : PAIR // 2])

        side_gamma = keep.tile([P, len(SIDE_HEADS) * HEAD // 2], F32)

        def copy_side_gamma(k):
            pair, second = divmod(SIDE_HEADS[k], 2)
            words = HEAD // 2
            nc.scalar.copy(
                out=side_gamma[:, k * words : (k + 1) * words],
                in_=gamma_banks[pair][:, second * words : (second + 1) * words],
            )

        turned_y = keep.tile([P, BANK], F32)
        turned_signed = keep.tile([P, 1], F32)

        def multiply_turned():
            j = TURNED
            z = psum.tile([P, BANK], F32, tag="bank")
            nc.tensor.matmul_mx(
                out=z[:],
                lhsT=w_codes[:, j * P : (j + 1) * P].bitcast(FP8X4),
                lhsT_scale=w_scales[:, j * P : (j + 1) * P],
                rhs=x_codes[:].bitcast(FP8X4), rhs_scale=x_scales[:],
                start=True, stop=True,
            )
            nc.scalar.activation(
                out=turned_y[:], in_=z[:], func=ACT.Identity,
                bias=turned_signed[:, 0:1], scale=sign[:, 0:1],
            )

        def turn():
            y_t = psum.tile([P, FREQ, P], F32, tag="bank")
            for f in range(FREQ):
                nc.tensor.transpose(y_t[:, f, :], turned_y[:, f * P : (f + 1) * P], ident[:])
            products[TURNED] = y_t

        def copy_turned():
            nc.scalar.copy(
                out=y[:, TURNED * BANK : (TURNED + 1) * BANK].rearrange("t (o f) -> t o f", f=FREQ),
                in_=products[TURNED][:].rearrange("t f o -> t o f"),
            )

        def activate_turned():
            cols = slice(*pieces[TURNED])
            nc.vector.scalar_tensor_tensor(
                out=prelu[:, cols].rearrange("t (o f) -> t o f", f=FREQ),
                in0=products[TURNED][:].rearrange("t f o -> t o f"), scalar=alpha_bc[:, 0:1],
                in1=y[:, cols].rearrange("t (o f) -> t o f", f=FREQ),
                op0=ALU.mult, op1=ALU.max, accum_out=sum_p[:, TURNED : TURNED + 1],
            )

        multiply(0)
        transpose_w(3)
        add_bias(0)
        quantise_w(2)
        multiply(1)
        transpose_w(4)
        nc.scalar.activation(
            out=turned_signed[:], in_=turned_bias[:], func=ACT.Copy, scale=sign[:, 0:1]
        )
        multiply_turned()
        add_bias(1)
        quantise_w(3)
        activate(0)
        multiply(3)
        transpose_w(5)
        quantise_w(4)
        activate(1)
        turn()
        copy_turned()
        add_bias(3)
        square(0)
        gamma_signed = signed_columns(gamma_cols, GAIN_ROWS, "gamma_signed")
        multiply(4)
        quantise_w(5)
        activate(3)
        square(1)
        activate_turned()
        add_bias(4)
        multiply(5)
        spread_gain_and_shift(gamma_signed)
        square(3)
        square(2)
        add_bias(5)
        for i in range(O_TILES - 2, n_pieces):
            activate(i)
            square(i)

        centred = keep.tile([P, COLS], F32)
        result = keep.tile([P, COLS], F32)
        neg_mean = keep.tile([P, 1], F32)
        offset_sq = keep.tile([P, 1], F32)
        mean_sq = keep.tile([P, 1], F32)
        scaled_sq = keep.tile([P, n_pieces + 1], F32)
        rstd = keep.tile([P, 1], F32)

        def gain(first, end):
            pair = first // PAIR
            words = gamma_banks[pair].bitcast(BF16)
            nc.vector.scalar_tensor_tensor(
                out=centred[:, first:end], in0=prelu[:, first:end], scalar=neg_mean[:, 0:1],
                in1=words[:, first - pair * PAIR : end - pair * PAIR],
                op0=ALU.add, op1=ALU.mult,
            )

        offsets = keep.tile([P, len(SIDE_HEADS) * HEAD], F32)

        def gain_beside(k):
            cols = slice(SIDE_HEADS[k] * HEAD, (SIDE_HEADS[k] + 1) * HEAD)
            side = slice(k * HEAD, (k + 1) * HEAD)
            if k == 0:
                nc.gpsimd.tensor_scalar(
                    out=offsets[:, side], in0=prelu[:, cols], scalar1=neg_mean[:, 0:1],
                    scalar2=1.0, op0=ALU.add, op1=ALU.mult,
                )
            else:
                nc.scalar.activation(
                    out=offsets[:, side], in_=prelu[:, cols],
                    func=ACT.Identity, bias=neg_mean[:, 0:1], scale=1.0,
                )
            nc.gpsimd.tensor_tensor(
                out=centred[:, cols], in0=offsets[:, side],
                in1=side_gamma[:].bitcast(BF16)[:, side], op=ALU.mult,
            )

        def add_shift(head):
            first, end = head * HEAD, (head + 1) * HEAD
            pair = head // 2
            words = beta_banks[pair].bitcast(BF16)
            nc.vector.scalar_tensor_tensor(
                out=result[:, first:end], in0=centred[:, first:end], scalar=rstd[:, 0:1],
                in1=words[:, first - pair * PAIR : end - pair * PAIR],
                op0=ALU.mult, op1=ALU.add,
            )

        by_kind = result[:].rearrange("t (h k d) -> t k h d", h=HEADS, k=3)

        def store(pair):
            heads = slice(2 * pair, 2 * pair + 2)
            for kind in range(3):
                nc.sync.dma_start(out=out_views[kind][:, heads, :], in_=by_kind[:, kind, heads, :])

        def gain_head(head):
            gain(head * HEAD, (head + 1) * HEAD)

        last = n_pieces - 1
        nc.vector.tensor_reduce(out=early_p[:], in_=sum_p[:, 0:last], axis=AXIS.X, op=ALU.add)
        nc.vector.tensor_scalar(
            out=neg_mean[:], in0=sum_p[:, last : last + 1], scalar1=early_p[:, 0:1],
            scalar2=-1.0 / COLS, op0=ALU.add, op1=ALU.mult,
        )
        nc.scalar.activation(
            out=offset_sq[:], in_=neg_mean[:], func=ACT.Square, bias=shift[:, 0:1], scale=1.0
        )
        copy_side_gamma(0)
        nc.scalar.activation(
            out=scaled_sq[:], in_=sum_sq[:], func=ACT.Identity, scale=1.0 / COLS,
            accum_out=mean_sq[:],
        )
        gain_head(0)
        gain_head(1)
        nc.scalar.activation(
            out=rstd[:], in_=offset_sq[:], func=ACT.Abs_reciprocal_sqrt,
            bias=mean_sq[:, 0:1], scale=-1.0,
        )
        gain_beside(0)
        copy_side_gamma(1)
        gain_beside(1)
        copy_side_gamma(2)
        gain_beside(2)
        copy_side_gamma(3)
        gain_beside(3)
        add_shift(0)
        add_shift(1)
        store(0)
        gain_head(3)
        add_shift(2)
        add_shift(3)
        store(1)
        gain_head(5)
        add_shift(4)
        add_shift(5)
        store(2)
        add_shift(6)
        add_shift(7)
        store(3)
